import numpy as np
import ml_dtypes


BF16 = ml_dtypes.bfloat16


def bf(x):
    return np.asarray(x, np.float32).astype(BF16)


def f64(x):
    return np.asarray(x).astype(np.float64)


E2M1 = np.array([0.0, 0.5, 1.0, 1.5, 2.0, 3.0, 4.0, 6.0, -0.0, -0.5, -1.0, -1.5, -2.0, -3.0, -4.0, -6.0])


def pack_weight(w, fmt):
    k, n = w.shape
    w = f64(bf(w)).reshape(k // 32, 32, n)
    amax = np.abs(w).max(1)
    if fmt == "e4m3":
        byte = np.frexp(amax)[1] - 1 + 127 - 7
    else:
        mant, ex = np.frexp(amax / 6.0)
        byte = np.where(mant > 0.5, ex, ex - 1) + 127
    byte = np.clip(np.where(amax > 0, byte, 1), 1, 254)
    scaled = (w * np.exp2(127.0 - byte)[:, None, :]).reshape(k, n).astype(np.float32)
    by_word = np.ascontiguousarray(scaled.reshape(k // 512, 128, 4, n).transpose(0, 1, 3, 2))
    if fmt == "e4m3":
        words = by_word.astype(ml_dtypes.float8_e4m3fn).view(np.uint8)
    else:
        c = by_word.astype(ml_dtypes.float4_e2m1fn).view(np.uint8) & 0xF
        words = c[..., 0::2] | (c[..., 1::2] << 4)
    return np.ascontiguousarray(words), np.ascontiguousarray(byte.astype(np.uint8).reshape(k // 512, 16, n))


def unpack_weight(words, scales, fmt):
    g, p, n, _ = words.shape
    if fmt == "e4m3":
        vals = np.ascontiguousarray(words).view(ml_dtypes.float8_e4m3fn).astype(np.float64)
    else:
        nib = np.empty((g, p, n, 4), np.uint8)
        nib[..., 0::2] = words & 0xF
        nib[..., 1::2] = words >> 4
        vals = E2M1[nib]
    vals = vals * np.repeat(np.exp2(scales.astype(np.float64) - 127.0), 8, axis=1)[..., None]
    return vals.transpose(0, 1, 3, 2).reshape(g * 512, n)

def pack4(w):
    words, scales = pack_weight(w, "e2m1")
    return words.reshape(words.shape[0], 128, -1), scales


def unpack4(words, scales):
    return unpack_weight(words.reshape(words.shape[0], 128, -1, 2), scales, "e2m1")


def kspread(k):
    return np.exp2(np.repeat(np.random.randint(-6, 7, k // 32), 32).astype(np.float64))


B, S, D, H, HS, R = 1, 128, 8192, 16, 64, 32
W = 3 * H * HS
HALF = R // 2
THETA = 10000.0


def rope_tables():
    inv = 1.0 / THETA ** (np.arange(0, R, 2) / R)
    pos = THETA - S + np.arange(S)
    ang = pos[:, None] * inv[None, :]
    return np.cos(ang), np.sin(ang)


def apply_rotary(t, cos, sin):
    re, im = t[..., :HALF], t[..., HALF:]
    c, sn = cos[None, :, None, :], sin[None, :, None, :]
    out = np.stack((re * c - im * sn, re * sn + im * c), axis=-1)
    return out.reshape(t.shape)


def setup_inputs():
    s = kspread(D)
    cos, sin = rope_tables()
    x = np.random.standard_normal((B, S, D)) * s
    x_words, x_scales = pack4(x.reshape(B * S, D).T)
    words, scales = pack4(np.random.standard_normal((D, W)) / np.sqrt(D) / s[:, None])
    b_qkv = bf(np.random.standard_normal(W) * 0.3)
    return {"x_words": x_words, "x_scales": x_scales,
            "w_qkv_words": words, "w_qkv_scales": scales,
            "b_qkv": b_qkv,
            "cos": bf(cos), "sin": bf(sin)}


def reference(x_words, x_scales, w_qkv_words, w_qkv_scales, b_qkv, cos, sin):
    cos, sin = f64(cos), f64(sin)
    x = unpack4(x_words, x_scales).T.reshape(B, S, D)
    qkv = (x @ unpack4(w_qkv_words, w_qkv_scales)) + f64(b_qkv)
    qkv = qkv.reshape(B, S, H, 3 * HS)
    q, k, v = qkv[..., :HS], qkv[..., HS:2 * HS], qkv[..., 2 * HS:]
    q_rot = np.concatenate((apply_rotary(q[..., :R], cos, sin), q[..., R:]), axis=3)
    k_rot = np.concatenate((apply_rotary(k[..., :R], cos, sin), k[..., R:]), axis=3)
    return q_rot, k_rot, v

@@ -1,0 +1,194 @@
+from contextlib import ExitStack
+
+import concourse.mybir as mybir
+
+F32 = mybir.dt.float32
+BF16 = mybir.dt.bfloat16
+I32 = mybir.dt.int32
+U8 = mybir.dt.uint8
+FP4X4 = mybir.dt.float4_e2m1fn_x4
+ADD = mybir.AluOpType.add
+MULT = mybir.AluOpType.mult
+
+P = 128
+PASSES = 16
+WIDTH = 3072
+HEADS = 16
+HS = 64
+ROT = 32
+HALF = 16
+NB = 512
+BANKS = 6
+SEGS = NB // HS
+
+FLOPS = 2 * 128 * 8192 * 3072
+
+ROW_PASSES = 11
+SCALE_RUNS = (((0, 2), (2, 4)), ((4, 6), (6, 8)), ((8, 9), (9, 11)), ((11, 13), (13, 16)))
+STORE_AFTER = (2, 4, 5)
+
+
+def tile_gptneoxattention_pa_kernel(
+    tc, x_words, x_scales, w_qkv_words, w_qkv_scales, b_qkv, cos, sin, out_0, out_1, out_2
+):
+    nc = tc.nc
+    outs = (out_0, out_1, out_2)
+
+    with ExitStack() as ctx:
+        keep = ctx.enter_context(tc.tile_pool(name="keep", bufs=1))
+        work = ctx.enter_context(tc.tile_pool(name="work", bufs=2))
+        psum = ctx.enter_context(tc.psum_pool(name="psum", bufs=1))
+        psum_b = ctx.enter_context(tc.psum_pool(name="psum_b", bufs=2))
+        ctx.enter_context(tc.manual_schedule())
+
+        xc = keep.tile([P, PASSES, 256], U8, name="xc", align_bytes=64)
+        xpl = keep.tile([P, PASSES, P], U8, name="xpl", align_bytes=64)
+        cos_sb = keep.tile([P, HALF], BF16, name="cos_sb")
+        sin_sb = keep.tile([P, HALF], BF16, name="sin_sb")
+        rot = keep.tile([P, ROT, 2], F32, name="rot")
+        brow = keep.tile([P, WIDTH], BF16, name="brow")
+        ones = keep.tile([P, P], BF16, name="ones")
+        bias = keep.tile([P, WIDTH], F32, name="bias")
+        res = keep.tile([P, 3, HEADS, HS], F32, name="res")
+        acc = []
+        for c in range(BANKS):
+            acc_c = psum.tile([P, NB], F32, name="acc%d" % c)
+            acc.append(acc_c)
+
+        plane_of = {}
+        plane_tiles = {}
+        for run in SCALE_RUNS:
+            for g0, g1 in run:
+                wpl = keep.tile([P, g1 - g0, WIDTH], U8, name="wpl%d" % g0, align_bytes=64)
+                plane_tiles[g0] = wpl
+                for g in range(g0, g1):
+                    plane_of[g] = (wpl, g - g0)
+
+        nc.scalar.dma_start(out=cos_sb[:], in_=cos)
+        nc.scalar.dma_start(out=sin_sb[:], in_=sin)
+
+        nc.vector.memset(xpl[:].bitcast(I32), 0)
+        first_run = True
+        for run in SCALE_RUNS:
+            for g0, g1 in run:
+                nc.vector.memset(plane_tiles[g0][:].bitcast(I32), 0)
+            if first_run:
+                nc.vector.memset(brow[:], 0.0)
+                nc.vector.memset(ones[:], 1.0)
+                first_run = False
+        nc.scalar.dma_start(out=brow[8:9, :], in_=b_qkv.rearrange("(o n) -> o n", o=1))
+
+        nc.vector.tensor_copy(out=rot[:, 0:HALF, 0], in_=cos_sb[:])
+        nc.vector.tensor_copy(out=rot[:, 0:HALF, 1], in_=sin_sb[:])
+        nc.vector.tensor_scalar(
+            out=rot[:, HALF:ROT, 0], in0=sin_sb[:], scalar1=-1.0, scalar2=None, op0=MULT
+        )
+        nc.vector.tensor_copy(out=rot[:, HALF:ROT, 1], in_=cos_sb[:])
+
+        def load_scales(planes, scales, g0, g1):
+            for r in range(4):
+                nc.sync.dma_start(
+                    out=planes[r:P:32, :, :].bitcast(I32),
+                    in_=scales[g0:g1, r:16:4, :].rearrange("g q n -> q g n").bitcast(I32),
+                )
+
+        row_codes = {}
+
+        def load_row(g):
+            wc = keep.tile([P, 2 * WIDTH], U8, name="wc%d" % g, align_bytes=64)
+            nc.sync.dma_start(out=wc[:].bitcast(I32), in_=w_qkv_words[g].bitcast(I32))
+            row_codes[g] = wc
+
+        nc.sync.dma_start(
+            out=xc[:].bitcast(I32), in_=x_words.rearrange("g p n -> p g n").bitcast(I32)
+        )
+        load_row(0)
+        load_scales(xpl, x_scales, 0, PASSES)
+        next_row = 1
+        for run in SCALE_RUNS:
+            for g0, g1 in run:
+                load_scales(plane_tiles[g0], w_qkv_scales, g0, g1)
+            run_end = run[-1][1]
+            while next_row < min(run_end, ROW_PASSES):
+                load_row(next_row)
+                next_row += 1
+
+        block_codes = []
+        for c in range(BANKS):
+            wb = keep.tile([P, PASSES - ROW_PASSES, 2 * NB], U8, name="wb%d" % c, align_bytes=64)
+            nc.sync.dma_start(
+                out=wb[:].bitcast(I32),
+                in_=w_qkv_words[ROW_PASSES:PASSES, :, 2 * NB * c : 2 * NB * (c + 1)]
+                .rearrange("g p n -> p g n")
+                .bitcast(I32),
+            )
+            block_codes.append(wb)
+
+        def multiply(g, c, codes):
+            planes, i = plane_of[g]
+            nc.tensor.matmul_mx(
+                out=acc[c][:],
+                lhsT=xc[:, g, :].bitcast(FP4X4),
+                lhsT_scale=xpl[:, g, :],
+                rhs=codes.bitcast(FP4X4),
+                rhs_scale=planes[:, i, NB * c : NB * (c + 1)],
+                start=(g == 0),
+                stop=(g == PASSES - 1),
+            )
+
+        for g in range(ROW_PASSES):
+            for c in range(BANKS):
+                multiply(g, c, row_codes[g][:, 2 * NB * c : 2 * NB * (c + 1)])
+            if g == 0:
+                for c in range(BANKS):
+                    bp = psum_b.tile([P, NB], F32, name="bp")
+                    nc.tensor.matmul(
+                        out=bp[:], lhsT=ones[:], rhs=brow[:, NB * c : NB * (c + 1)], start=True, stop=True
+                    )
+                    nc.scalar.copy(out=bias[:, NB * c : NB * (c + 1)], in_=bp[:])
+
+        stored = [0, 0, 0]
+        for c in range(BANKS):
+            for g in range(ROW_PASSES, PASSES):
+                multiply(g, c, block_codes[c][:, g - ROW_PASSES, :])
+
+            acc_seg = acc[c][:].rearrange("p (s f) -> p s f", f=HS)
+            bias_seg = bias[:, NB * c : NB * (c + 1)].rearrange("p (s f) -> p s f", f=HS)
+            spans = {}
+            for t in range(3):
+                first = (t - SEGS * c) % 3
+                nh = len(range(first, SEGS, 3))
+                h0 = (SEGS * c + first) // 3
+                spans[t] = (h0, nh)
+                nc.vector.tensor_tensor(
+                    out=res[:, t, h0 : h0 + nh, :],
+                    in0=acc_seg[:, first:SEGS:3, :],
+                    in1=bias_seg[:, first:SEGS:3, :],
+                    op=ADD,
+                )
+            prods = {}
+            for t in range(2):
+                h0, nh = spans[t]
+                prod = work.tile([P, 3, ROT, 2], F32, name="prod%d" % t)
+                nc.vector.tensor_tensor(
+                    out=prod[:, 0:nh, :, :],
+                    in0=res[:, t, h0 : h0 + nh, 0:ROT].unsqueeze(3).to_broadcast([P, nh, ROT, 2]),
+                    in1=rot[:].unsqueeze(1).to_broadcast([P, nh, ROT, 2]),
+                    op=MULT,
+                )
+                prods[t] = prod
+            for t in range(2):
+                h0, nh = spans[t]
+                nc.vector.tensor_tensor(
+                    out=res[:, t, h0 : h0 + nh, 0:ROT].rearrange("p h (j e) -> p h j e", e=2),
+                    in0=prods[t][:, 0:nh, 0:HALF, :],
+                    in1=prods[t][:, 0:nh, HALF:ROT, :],
+                    op=ADD,
+                )
+            if c in STORE_AFTER:
+                for t, queue in ((2, nc.scalar), (0, nc.sync), (1, nc.scalar)):
+                    h1 = spans[t][0] + spans[t][1]
+                    queue.dma_start(
+                        out=outs[t][0, :, stored[t] : h1, :], in_=res[:, t, stored[t] : h1, :]
+                    )
+                    stored[t] = h1

@@ -18,14 +18,15 @@ HS = 64
 ROT = 32
 HALF = 16
 NB = 512
-BANKS = 6
-SEGS = NB // HS
 
 FLOPS = 2 * 128 * 8192 * 3072
 
+GROUPS = ((0, 512), (512, 512), (1024, 512), (1536, 512), (2048, 512), (2560, 256), (2816, 256))
 ROW_PASSES = 11
-SCALE_RUNS = (((0, 2), (2, 4)), ((4, 6), (6, 8)), ((8, 9), (9, 11)), ((11, 13), (13, 16)))
-STORE_AFTER = (2, 4, 5)
+PRELOAD = 3
+SCALE_RUNS = (((0, 2), (2, 4), (4, 6), (6, 8), (8, 10), (10, 12), (12, 14), (14, 15), (15, 16)),)
+BLOCK_SPLITS = (((11, 16),), ((11, 16),), ((11, 16),), ((11, 16),), ((11, 16),), ((11, 16),), ((11, 14), (14, 16)))
+STORE_AFTER = (2, 4, 5, 6)
 
 
 def tile_gptneoxattention_pa_kernel(
@@ -38,7 +39,6 @@ def tile_gptneoxattention_pa_kernel(
         keep = ctx.enter_context(tc.tile_pool(name="keep", bufs=1))
         work = ctx.enter_context(tc.tile_pool(name="work", bufs=2))
         psum = ctx.enter_context(tc.psum_pool(name="psum", bufs=1))
-        psum_b = ctx.enter_context(tc.psum_pool(name="psum_b", bufs=2))
         ctx.enter_context(tc.manual_schedule())
 
         xc = keep.tile([P, PASSES, 256], U8, name="xc", align_bytes=64)
@@ -51,8 +51,8 @@ def tile_gptneoxattention_pa_kernel(
         bias = keep.tile([P, WIDTH], F32, name="bias")
         res = keep.tile([P, 3, HEADS, HS], F32, name="res")
         acc = []
-        for c in range(BANKS):
-            acc_c = psum.tile([P, NB], F32, name="acc%d" % c)
+        for c in range(len(GROUPS)):
+            acc_c = psum.tile([P, GROUPS[c][1]], F32, name="acc%d" % c)
             acc.append(acc_c)
 
         plane_of = {}
@@ -68,14 +68,14 @@ def tile_gptneoxattention_pa_kernel(
         nc.scalar.dma_start(out=sin_sb[:], in_=sin)
 
         nc.vector.memset(xpl[:].bitcast(I32), 0)
-        first_run = True
+        filled = 0
         for run in SCALE_RUNS:
             for g0, g1 in run:
                 nc.vector.memset(plane_tiles[g0][:].bitcast(I32), 0)
-            if first_run:
-                nc.vector.memset(brow[:], 0.0)
-                nc.vector.memset(ones[:], 1.0)
-                first_run = False
+                filled += 1
+                if filled == 2:
+                    nc.vector.memset(brow[:], 0.0)
+                    nc.vector.memset(ones[:], 1.0)
         nc.scalar.dma_start(out=brow[8:9, :], in_=b_qkv.rearrange("(o n) -> o n", o=1))
 
         nc.vector.tensor_copy(out=rot[:, 0:HALF, 0], in_=cos_sb[:])
@@ -102,9 +102,10 @@ def tile_gptneoxattention_pa_kernel(
         nc.sync.dma_start(
             out=xc[:].bitcast(I32), in_=x_words.rearrange("g p n -> p g n").bitcast(I32)
         )
-        load_row(0)
+        for g in range(PRELOAD):
+            load_row(g)
         load_scales(xpl, x_scales, 0, PASSES)
-        next_row = 1
+        next_row = PRELOAD
         for run in SCALE_RUNS:
             for g0, g1 in run:
                 load_scales(plane_tiles[g0], w_qkv_scales, g0, g1)
@@ -113,57 +114,65 @@ def tile_gptneoxattention_pa_kernel(
                 load_row(next_row)
                 next_row += 1
 
-        block_codes = []
-        for c in range(BANKS):
-            wb = keep.tile([P, PASSES - ROW_PASSES, 2 * NB], U8, name="wb%d" % c, align_bytes=64)
-            nc.sync.dma_start(
-                out=wb[:].bitcast(I32),
-                in_=w_qkv_words[ROW_PASSES:PASSES, :, 2 * NB * c : 2 * NB * (c + 1)]
-                .rearrange("g p n -> p g n")
-                .bitcast(I32),
-            )
-            block_codes.append(wb)
+        block_codes = {}
+        for c in range(len(GROUPS)):
+            col0, ncol = GROUPS[c]
+            for g0, g1 in BLOCK_SPLITS[c]:
+                wb = keep.tile([P, g1 - g0, 2 * ncol], U8, name="wb%d_%d" % (c, g0), align_bytes=64)
+                nc.sync.dma_start(
+                    out=wb[:].bitcast(I32),
+                    in_=w_qkv_words[g0:g1, :, 2 * col0 : 2 * (col0 + ncol)]
+                    .rearrange("g p n -> p g n")
+                    .bitcast(I32),
+                )
+                for g in range(g0, g1):
+                    block_codes[(c, g)] = wb[:, g - g0, :]
 
         def multiply(g, c, codes):
             planes, i = plane_of[g]
+            col0, ncol = GROUPS[c]
             nc.tensor.matmul_mx(
                 out=acc[c][:],
                 lhsT=xc[:, g, :].bitcast(FP4X4),
                 lhsT_scale=xpl[:, g, :],
                 rhs=codes.bitcast(FP4X4),
-                rhs_scale=planes[:, i, NB * c : NB * (c + 1)],
+                rhs_scale=planes[:, i, col0 : col0 + ncol],
                 start=(g == 0),
                 stop=(g == PASSES - 1),
             )
 
         for g in range(ROW_PASSES):
-            for c in range(BANKS):
-                multiply(g, c, row_codes[g][:, 2 * NB * c : 2 * NB * (c + 1)])
+            for c in range(len(GROUPS)):
+                col0, ncol = GROUPS[c]
+                multiply(g, c, row_codes[g][:, 2 * col0 : 2 * (col0 + ncol)])
             if g == 0:
-                for c in range(BANKS):
-                    bp = psum_b.tile([P, NB], F32, name="bp")
+                for i in range(WIDTH // NB):
+                    bp = psum.tile([P, NB], F32, name="bp")
                     nc.tensor.matmul(
-                        out=bp[:], lhsT=ones[:], rhs=brow[:, NB * c : NB * (c + 1)], start=True, stop=True
+                        out=bp[:], lhsT=ones[:], rhs=brow[:, NB * i : NB * (i + 1)], start=True, stop=True
                     )
-                    nc.scalar.copy(out=bias[:, NB * c : NB * (c + 1)], in_=bp[:])
+                    nc.scalar.copy(out=bias[:, NB * i : NB * (i + 1)], in_=bp[:])
 
         stored = [0, 0, 0]
-        for c in range(BANKS):
+        for c in range(len(GROUPS)):
+            col0, ncol = GROUPS[c]
             for g in range(ROW_PASSES, PASSES):
-                multiply(g, c, block_codes[c][:, g - ROW_PASSES, :])
+                multiply(g, c, block_codes[(c, g)])
 
+            seg0 = col0 // HS
+            nseg = ncol // HS
             acc_seg = acc[c][:].rearrange("p (s f) -> p s f", f=HS)
-            bias_seg = bias[:, NB * c : NB * (c + 1)].rearrange("p (s f) -> p s f", f=HS)
+            bias_seg = bias[:, col0 : col0 + ncol].rearrange("p (s f) -> p s f", f=HS)
             spans = {}
             for t in range(3):
-                first = (t - SEGS * c) % 3
-                nh = len(range(first, SEGS, 3))
-                h0 = (SEGS * c + first) // 3
+                first = (t - seg0) % 3
+                nh = len(range(first, nseg, 3))
+                h0 = (seg0 + first) // 3
                 spans[t] = (h0, nh)
                 nc.vector.tensor_tensor(
                     out=res[:, t, h0 : h0 + nh, :],
-                    in0=acc_seg[:, first:SEGS:3, :],
-                    in1=bias_seg[:, first:SEGS:3, :],
+                    in0=acc_seg[:, first:nseg:3, :],
+                    in1=bias_seg[:, first:nseg:3, :],
                     op=ADD,
                 )
             prods = {}

@@ -21,12 +21,11 @@ NB = 512
 
 FLOPS = 2 * 128 * 8192 * 3072
 
-GROUPS = ((0, 512), (512, 512), (1024, 512), (1536, 512), (2048, 512), (2560, 256), (2816, 256))
+GROUPS = ((0, 512), (512, 512), (1024, 512), (1536, 512), (2048, 512), (2560, 512))
 ROW_PASSES = 11
-PRELOAD = 3
-SCALE_RUNS = (((0, 2), (2, 4), (4, 6), (6, 8), (8, 10), (10, 12), (12, 14), (14, 15), (15, 16)),)
-BLOCK_SPLITS = (((11, 16),), ((11, 16),), ((11, 16),), ((11, 16),), ((11, 16),), ((11, 16),), ((11, 14), (14, 16)))
-STORE_AFTER = (2, 4, 5, 6)
+LOAD_PLAN = (("x",), ("xs",), ("scales_sync", 0, 2), ("scales", 2, 4), ("scales", 4, 8), ("scales", 8, 12), ("scales", 12, 16), ("rows", 0, 1), ("rows", 1, 2), ("rows", 2, 3), ("rows", 3, 5), ("rows", 5, 7), ("rows", 7, 9), ("rows", 9, 11), ("block", 0, 11, 16), ("block", 1, 11, 16), ("block", 2, 11, 16), ("block", 3, 11, 16), ("block", 4, 11, 16), ("block", 5, 11, 16))
+STORE_AFTER = (2, 4, 5)
+STORE_QUEUES = {2: ("sync", "sync", "sync"), 4: ("sync", "sync", "sync"), 5: ("sync", "sync", "sync")}
 
 
 def tile_gptneoxattention_pa_kernel(
@@ -34,6 +33,7 @@ def tile_gptneoxattention_pa_kernel(
 ):
     nc = tc.nc
     outs = (out_0, out_1, out_2)
+    queues = {"sync": nc.sync, "scalar": nc.scalar}
 
     with ExitStack() as ctx:
         keep = ctx.enter_context(tc.tile_pool(name="keep", bufs=1))
@@ -55,23 +55,21 @@ def tile_gptneoxattention_pa_kernel(
             acc_c = psum.tile([P, GROUPS[c][1]], F32, name="acc%d" % c)
             acc.append(acc_c)
 
+        nc.scalar.dma_start(out=cos_sb[:], in_=cos)
+        nc.scalar.dma_start(out=sin_sb[:], in_=sin)
+
         plane_of = {}
         plane_tiles = {}
-        for run in SCALE_RUNS:
-            for g0, g1 in run:
+        nc.vector.memset(xpl[:].bitcast(I32), 0)
+        filled = 0
+        for step in LOAD_PLAN:
+            if step[0] in ("scales", "scales_sync"):
+                g0, g1 = step[1], step[2]
                 wpl = keep.tile([P, g1 - g0, WIDTH], U8, name="wpl%d" % g0, align_bytes=64)
                 plane_tiles[g0] = wpl
                 for g in range(g0, g1):
                     plane_of[g] = (wpl, g - g0)
-
-        nc.scalar.dma_start(out=cos_sb[:], in_=cos)
-        nc.scalar.dma_start(out=sin_sb[:], in_=sin)
-
-        nc.vector.memset(xpl[:].bitcast(I32), 0)
-        filled = 0
-        for run in SCALE_RUNS:
-            for g0, g1 in run:
-                nc.vector.memset(plane_tiles[g0][:].bitcast(I32), 0)
+                nc.vector.memset(wpl[:].bitcast(I32), 0)
                 filled += 1
                 if filled == 2:
                     nc.vector.memset(brow[:], 0.0)
@@ -85,39 +83,39 @@ def tile_gptneoxattention_pa_kernel(
         )
         nc.vector.tensor_copy(out=rot[:, HALF:ROT, 1], in_=cos_sb[:])
 
-        def load_scales(planes, scales, g0, g1):
+        def load_scales(planes, scales, g0, g1, queue, view):
             for r in range(4):
-                nc.sync.dma_start(
-                    out=planes[r:P:32, :, :].bitcast(I32),
-                    in_=scales[g0:g1, r:16:4, :].rearrange("g q n -> q g n").bitcast(I32),
+                queue.dma_start(
+                    out=planes[r:P:32, :, :].bitcast(view),
+                    in_=scales[g0:g1, r:16:4, :].rearrange("g q n -> q g n").bitcast(view),
                 )
 
-        row_codes = {}
-
-        def load_row(g):
-            wc = keep.tile([P, 2 * WIDTH], U8, name="wc%d" % g, align_bytes=64)
-            nc.sync.dma_start(out=wc[:].bitcast(I32), in_=w_qkv_words[g].bitcast(I32))
-            row_codes[g] = wc
-
-        nc.sync.dma_start(
-            out=xc[:].bitcast(I32), in_=x_words.rearrange("g p n -> p g n").bitcast(I32)
-        )
-        for g in range(PRELOAD):
-            load_row(g)
-        load_scales(xpl, x_scales, 0, PASSES)
-        next_row = PRELOAD
-        for run in SCALE_RUNS:
-            for g0, g1 in run:
-                load_scales(plane_tiles[g0], w_qkv_scales, g0, g1)
-            run_end = run[-1][1]
-            while next_row < min(run_end, ROW_PASSES):
-                load_row(next_row)
-                next_row += 1
-
-        block_codes = {}
-        for c in range(len(GROUPS)):
-            col0, ncol = GROUPS[c]
-            for g0, g1 in BLOCK_SPLITS[c]:
+        codes_of = {}
+        for step in LOAD_PLAN:
+            if step[0] == "x":
+                nc.sync.dma_start(
+                    out=xc[:].bitcast(I32), in_=x_words.rearrange("g p n -> p g n").bitcast(I32)
+                )
+            elif step[0] == "xs":
+                load_scales(xpl, x_scales, 0, PASSES, nc.sync, I32)
+            elif step[0] == "scales_sync":
+                load_scales(plane_tiles[step[1]], w_qkv_scales, step[1], step[2], nc.sync, I32)
+            elif step[0] == "scales":
+                load_scales(plane_tiles[step[1]], w_qkv_scales, step[1], step[2], nc.gpsimd, F32)
+            elif step[0] == "rows":
+                g0, g1 = step[1], step[2]
+                wc = keep.tile([P, g1 - g0, 2 * WIDTH], U8, name="wc%d" % g0, align_bytes=64)
+                nc.sync.dma_start(
+                    out=wc[:].bitcast(I32),
+                    in_=w_qkv_words[g0:g1].rearrange("g p n -> p g n").bitcast(I32),
+                )
+                for g in range(g0, g1):
+                    for c in range(len(GROUPS)):
+                        col0, ncol = GROUPS[c]
+                        codes_of[(c, g)] = wc[:, g - g0, 2 * col0 : 2 * (col0 + ncol)]
+            else:
+                c, g0, g1 = step[1], step[2], step[3]
+                col0, ncol = GROUPS[c]
                 wb = keep.tile([P, g1 - g0, 2 * ncol], U8, name="wb%d_%d" % (c, g0), align_bytes=64)
                 nc.sync.dma_start(
                     out=wb[:].bitcast(I32),
@@ -126,16 +124,16 @@ def tile_gptneoxattention_pa_kernel(
                     .bitcast(I32),
                 )
                 for g in range(g0, g1):
-                    block_codes[(c, g)] = wb[:, g - g0, :]
+                    codes_of[(c, g)] = wb[:, g - g0, :]
 
-        def multiply(g, c, codes):
+        def multiply(g, c):
             planes, i = plane_of[g]
             col0, ncol = GROUPS[c]
             nc.tensor.matmul_mx(
                 out=acc[c][:],
                 lhsT=xc[:, g, :].bitcast(FP4X4),
                 lhsT_scale=xpl[:, g, :],
-                rhs=codes.bitcast(FP4X4),
+                rhs=codes_of[(c, g)].bitcast(FP4X4),
                 rhs_scale=planes[:, i, col0 : col0 + ncol],
                 start=(g == 0),
                 stop=(g == PASSES - 1),
@@ -143,8 +141,7 @@ def tile_gptneoxattention_pa_kernel(
 
         for g in range(ROW_PASSES):
             for c in range(len(GROUPS)):
-                col0, ncol = GROUPS[c]
-                multiply(g, c, row_codes[g][:, 2 * col0 : 2 * (col0 + ncol)])
+                multiply(g, c)
             if g == 0:
                 for i in range(WIDTH // NB):
                     bp = psum.tile([P, NB], F32, name="bp")
@@ -157,14 +154,14 @@ def tile_gptneoxattention_pa_kernel(
         for c in range(len(GROUPS)):
             col0, ncol = GROUPS[c]
             for g in range(ROW_PASSES, PASSES):
-                multiply(g, c, block_codes[(c, g)])
+                multiply(g, c)
 
             seg0 = col0 // HS
             nseg = ncol // HS
             acc_seg = acc[c][:].rearrange("p (s f) -> p s f", f=HS)
             bias_seg = bias[:, col0 : col0 + ncol].rearrange("p (s f) -> p s f", f=HS)
             spans = {}
-            for t in range(3):
+            for t in (2, 0, 1):
                 first = (t - seg0) % 3
                 nh = len(range(first, nseg, 3))
                 h0 = (seg0 + first) // 3
@@ -195,9 +192,9 @@ def tile_gptneoxattention_pa_kernel(
                     op=ADD,
                 )
             if c in STORE_AFTER:
-                for t, queue in ((2, nc.scalar), (0, nc.sync), (1, nc.scalar)):
+                for t in (2, 0, 1):
                     h1 = spans[t][0] + spans[t][1]
-                    queue.dma_start(
+                    queues[STORE_QUEUES[c][t]].dma_start(
                         out=outs[t][0, :, stored[t] : h1, :], in_=res[:, t, stored[t] : h1, :]
                     )
                     stored[t] = h1

@@ -22,10 +22,10 @@ NB = 512
 FLOPS = 2 * 128 * 8192 * 3072
 
 GROUPS = ((0, 512), (512, 512), (1024, 512), (1536, 512), (2048, 512), (2560, 512))
-ROW_PASSES = 11
-LOAD_PLAN = (("x",), ("xs",), ("scales_sync", 0, 2), ("scales", 2, 4), ("scales", 4, 8), ("scales", 8, 12), ("scales", 12, 16), ("rows", 0, 1), ("rows", 1, 2), ("rows", 2, 3), ("rows", 3, 5), ("rows", 5, 7), ("rows", 7, 9), ("rows", 9, 11), ("block", 0, 11, 16), ("block", 1, 11, 16), ("block", 2, 11, 16), ("block", 3, 11, 16), ("block", 4, 11, 16), ("block", 5, 11, 16))
+ROW_PASSES = 12
+LOAD_PLAN = (("x",), ("rows", 0, 2), ("xs",), ("scales", 0, 4), ("rows", 2, 4), ("scales", 4, 8), ("rows", 4, 6), ("rows", 6, 8), ("scales", 8, 12), ("rows", 8, 10), ("rows", 10, 12), ("scales", 12, 16), ("block", 0, 12, 16), ("block", 1, 12, 16), ("block", 2, 12, 16), ("block", 3, 12, 16), ("block", 4, 12, 16), ("block", 5, 12, 16))
 STORE_AFTER = (2, 4, 5)
-STORE_QUEUES = {2: ("sync", "sync", "sync"), 4: ("sync", "sync", "sync"), 5: ("sync", "sync", "sync")}
+STORE_QUEUES = {2: ("sync", "scalar", "scalar"), 4: ("sync", "scalar", "scalar"), 5: ("sync", "scalar", "scalar")}
 
 
 def tile_gptneoxattention_pa_kernel(
@@ -63,7 +63,7 @@ def tile_gptneoxattention_pa_kernel(
         nc.vector.memset(xpl[:].bitcast(I32), 0)
         filled = 0
         for step in LOAD_PLAN:
-            if step[0] in ("scales", "scales_sync"):
+            if step[0] == "scales":
                 g0, g1 = step[1], step[2]
                 wpl = keep.tile([P, g1 - g0, WIDTH], U8, name="wpl%d" % g0, align_bytes=64)
                 plane_tiles[g0] = wpl
@@ -83,11 +83,11 @@ def tile_gptneoxattention_pa_kernel(
         )
         nc.vector.tensor_copy(out=rot[:, HALF:ROT, 1], in_=cos_sb[:])
 
-        def load_scales(planes, scales, g0, g1, queue, view):
+        def load_scales(planes, scales, g0, g1):
             for r in range(4):
-                queue.dma_start(
-                    out=planes[r:P:32, :, :].bitcast(view),
-                    in_=scales[g0:g1, r:16:4, :].rearrange("g q n -> q g n").bitcast(view),
+                nc.sync.dma_start(
+                    out=planes[r:P:32, :, :].bitcast(I32),
+                    in_=scales[g0:g1, r:16:4, :].rearrange("g q n -> q g n").bitcast(I32),
                 )
 
         codes_of = {}
@@ -97,11 +97,9 @@ def tile_gptneoxattention_pa_kernel(
                     out=xc[:].bitcast(I32), in_=x_words.rearrange("g p n -> p g n").bitcast(I32)
                 )
             elif step[0] == "xs":
-                load_scales(xpl, x_scales, 0, PASSES, nc.sync, I32)
-            elif step[0] == "scales_sync":
-                load_scales(plane_tiles[step[1]], w_qkv_scales, step[1], step[2], nc.sync, I32)
+                load_scales(xpl, x_scales, 0, PASSES)
             elif step[0] == "scales":
-                load_scales(plane_tiles[step[1]], w_qkv_scales, step[1], step[2], nc.gpsimd, F32)
+                load_scales(plane_tiles[step[1]], w_qkv_scales, step[1], step[2])
             elif step[0] == "rows":
                 g0, g1 = step[1], step[2]
                 wc = keep.tile([P, g1 - g0, 2 * WIDTH], U8, name="wc%d" % g0, align_bytes=64)

@@ -14,18 +14,22 @@ P = 128
 PASSES = 16
 WIDTH = 3072
 HEADS = 16
-HS = 64
-ROT = 32
-HALF = 16
-NB = 512
+HEAD_SIZE = 64
+ROTARY = 32
+HALF = ROTARY // 2
+QUERY, KEY, VALUE = 0, 1, 2
+BANK = 512
+BANKS = WIDTH // BANK
+SEGMENTS = BANK // HEAD_SIZE
 
-FLOPS = 2 * 128 * 8192 * 3072
+FLOPS = 2 * P * 512 * PASSES * WIDTH
 
-GROUPS = ((0, 512), (512, 512), (1024, 512), (1536, 512), (2048, 512), (2560, 512))
-ROW_PASSES = 12
-LOAD_PLAN = (("x",), ("rows", 0, 2), ("xs",), ("scales", 0, 4), ("rows", 2, 4), ("scales", 4, 8), ("rows", 4, 6), ("rows", 6, 8), ("scales", 8, 12), ("rows", 8, 10), ("rows", 10, 12), ("scales", 12, 16), ("block", 0, 12, 16), ("block", 1, 12, 16), ("block", 2, 12, 16), ("block", 3, 12, 16), ("block", 4, 12, 16), ("block", 5, 12, 16))
+ROW_PASSES = 11
+FIRST_X_PASSES = 4
+SYNC_SCALES = ((0, 1), (1, 2))
+GPSIMD_SCALES = ((2, 4), (4, 8))
+LATE_GPSIMD_SCALES = {0: (8, 12), 2: (12, 16)}
 STORE_AFTER = (2, 4, 5)
-STORE_QUEUES = {2: ("sync", "scalar", "scalar"), 4: ("sync", "scalar", "scalar"), 5: ("sync", "scalar", "scalar")}
 
 
 def tile_gptneoxattention_pa_kernel(
@@ -33,166 +37,177 @@ def tile_gptneoxattention_pa_kernel(
 ):
     nc = tc.nc
     outs = (out_0, out_1, out_2)
-    queues = {"sync": nc.sync, "scalar": nc.scalar}
 
     with ExitStack() as ctx:
         keep = ctx.enter_context(tc.tile_pool(name="keep", bufs=1))
         work = ctx.enter_context(tc.tile_pool(name="work", bufs=2))
         psum = ctx.enter_context(tc.psum_pool(name="psum", bufs=1))
+        psum_bias = ctx.enter_context(tc.psum_pool(name="psum_bias", bufs=2))
         ctx.enter_context(tc.manual_schedule())
 
-        xc = keep.tile([P, PASSES, 256], U8, name="xc", align_bytes=64)
-        xpl = keep.tile([P, PASSES, P], U8, name="xpl", align_bytes=64)
+        x_codes = keep.tile([P, PASSES, 2 * P], U8, name="x_codes", align_bytes=64)
+        x_planes = keep.tile([P, PASSES, P], U8, name="x_planes", align_bytes=64)
         cos_sb = keep.tile([P, HALF], BF16, name="cos_sb")
         sin_sb = keep.tile([P, HALF], BF16, name="sin_sb")
-        rot = keep.tile([P, ROT, 2], F32, name="rot")
-        brow = keep.tile([P, WIDTH], BF16, name="brow")
+        rotation = keep.tile([P, ROTARY, 2], F32, name="rotation")
+        bias_row = keep.tile([P, WIDTH], BF16, name="bias_row")
         ones = keep.tile([P, P], BF16, name="ones")
         bias = keep.tile([P, WIDTH], F32, name="bias")
-        res = keep.tile([P, 3, HEADS, HS], F32, name="res")
+        result = keep.tile([P, 3, HEADS, HEAD_SIZE], F32, name="result")
         acc = []
-        for c in range(len(GROUPS)):
-            acc_c = psum.tile([P, GROUPS[c][1]], F32, name="acc%d" % c)
+        for c in range(BANKS):
+            acc_c = psum.tile([P, BANK], F32, name="acc%d" % c)
             acc.append(acc_c)
 
-        nc.scalar.dma_start(out=cos_sb[:], in_=cos)
-        nc.scalar.dma_start(out=sin_sb[:], in_=sin)
+        w_plane = {}
+        w_codes = {}
 
-        plane_of = {}
-        plane_tiles = {}
-        nc.vector.memset(xpl[:].bitcast(I32), 0)
-        filled = 0
-        for step in LOAD_PLAN:
-            if step[0] == "scales":
-                g0, g1 = step[1], step[2]
-                wpl = keep.tile([P, g1 - g0, WIDTH], U8, name="wpl%d" % g0, align_bytes=64)
-                plane_tiles[g0] = wpl
-                for g in range(g0, g1):
-                    plane_of[g] = (wpl, g - g0)
-                nc.vector.memset(wpl[:].bitcast(I32), 0)
-                filled += 1
-                if filled == 2:
-                    nc.vector.memset(brow[:], 0.0)
-                    nc.vector.memset(ones[:], 1.0)
-        nc.scalar.dma_start(out=brow[8:9, :], in_=b_qkv.rearrange("(o n) -> o n", o=1))
+        def new_planes(g0, g1):
+            planes = keep.tile([P, g1 - g0, WIDTH], U8, name="w_planes%d" % g0, align_bytes=64)
+            nc.vector.memset(planes[:].bitcast(I32), 0)
+            for g in range(g0, g1):
+                w_plane[g] = planes[:, g - g0, :]
+            return planes
 
-        nc.vector.tensor_copy(out=rot[:, 0:HALF, 0], in_=cos_sb[:])
-        nc.vector.tensor_copy(out=rot[:, 0:HALF, 1], in_=sin_sb[:])
-        nc.vector.tensor_scalar(
-            out=rot[:, HALF:ROT, 0], in0=sin_sb[:], scalar1=-1.0, scalar2=None, op0=MULT
-        )
-        nc.vector.tensor_copy(out=rot[:, HALF:ROT, 1], in_=cos_sb[:])
-
-        def load_scales(planes, scales, g0, g1):
+        def load_scale_rows(queue, word, planes, scales, g0, g1):
             for r in range(4):
-                nc.sync.dma_start(
-                    out=planes[r:P:32, :, :].bitcast(I32),
-                    in_=scales[g0:g1, r:16:4, :].rearrange("g q n -> q g n").bitcast(I32),
+                queue.dma_start(
+                    out=planes[r:P:32, :, :].bitcast(word),
+                    in_=scales[g0:g1, r:16:4, :].rearrange("g q n -> q g n").bitcast(word),
                 )
 
-        codes_of = {}
-        for step in LOAD_PLAN:
-            if step[0] == "x":
-                nc.sync.dma_start(
-                    out=xc[:].bitcast(I32), in_=x_words.rearrange("g p n -> p g n").bitcast(I32)
-                )
-            elif step[0] == "xs":
-                load_scales(xpl, x_scales, 0, PASSES)
-            elif step[0] == "scales":
-                load_scales(plane_tiles[step[1]], w_qkv_scales, step[1], step[2])
-            elif step[0] == "rows":
-                g0, g1 = step[1], step[2]
-                wc = keep.tile([P, g1 - g0, 2 * WIDTH], U8, name="wc%d" % g0, align_bytes=64)
-                nc.sync.dma_start(
-                    out=wc[:].bitcast(I32),
-                    in_=w_qkv_words[g0:g1].rearrange("g p n -> p g n").bitcast(I32),
-                )
-                for g in range(g0, g1):
-                    for c in range(len(GROUPS)):
-                        col0, ncol = GROUPS[c]
-                        codes_of[(c, g)] = wc[:, g - g0, 2 * col0 : 2 * (col0 + ncol)]
-            else:
-                c, g0, g1 = step[1], step[2], step[3]
-                col0, ncol = GROUPS[c]
-                wb = keep.tile([P, g1 - g0, 2 * ncol], U8, name="wb%d_%d" % (c, g0), align_bytes=64)
-                nc.sync.dma_start(
-                    out=wb[:].bitcast(I32),
-                    in_=w_qkv_words[g0:g1, :, 2 * col0 : 2 * (col0 + ncol)]
-                    .rearrange("g p n -> p g n")
-                    .bitcast(I32),
-                )
-                for g in range(g0, g1):
-                    codes_of[(c, g)] = wb[:, g - g0, :]
+        def load_x_codes(g0, g1):
+            nc.sync.dma_start(
+                out=x_codes[:, g0:g1, :].bitcast(I32),
+                in_=x_words[g0:g1].rearrange("g p n -> p g n").bitcast(I32),
+            )
+
+        def load_row_pass(g):
+            codes = keep.tile([P, 2 * WIDTH], U8, name="w_row%d" % g, align_bytes=64)
+            nc.sync.dma_start(out=codes[:].bitcast(I32), in_=w_qkv_words[g].bitcast(I32))
+            for c in range(BANKS):
+                w_codes[(c, g)] = codes[:, 2 * BANK * c : 2 * BANK * (c + 1)]
+
+        def load_bank_passes(c):
+            codes = keep.tile([P, PASSES - ROW_PASSES, 2 * BANK], U8, name="w_bank%d" % c, align_bytes=64)
+            nc.sync.dma_start(
+                out=codes[:].bitcast(I32),
+                in_=w_qkv_words[ROW_PASSES:PASSES, :, 2 * BANK * c : 2 * BANK * (c + 1)]
+                .rearrange("g p n -> p g n")
+                .bitcast(I32),
+            )
+            for g in range(ROW_PASSES, PASSES):
+                w_codes[(c, g)] = codes[:, g - ROW_PASSES, :]
 
         def multiply(g, c):
-            planes, i = plane_of[g]
-            col0, ncol = GROUPS[c]
             nc.tensor.matmul_mx(
                 out=acc[c][:],
-                lhsT=xc[:, g, :].bitcast(FP4X4),
-                lhsT_scale=xpl[:, g, :],
-                rhs=codes_of[(c, g)].bitcast(FP4X4),
-                rhs_scale=planes[:, i, col0 : col0 + ncol],
+                lhsT=x_codes[:, g, :].bitcast(FP4X4),
+                lhsT_scale=x_planes[:, g, :],
+                rhs=w_codes[(c, g)].bitcast(FP4X4),
+                rhs_scale=w_plane[g][:, BANK * c : BANK * (c + 1)],
                 start=(g == 0),
                 stop=(g == PASSES - 1),
             )
 
-        for g in range(ROW_PASSES):
-            for c in range(len(GROUPS)):
-                multiply(g, c)
-            if g == 0:
-                for i in range(WIDTH // NB):
-                    bp = psum.tile([P, NB], F32, name="bp")
-                    nc.tensor.matmul(
-                        out=bp[:], lhsT=ones[:], rhs=brow[:, NB * i : NB * (i + 1)], start=True, stop=True
-                    )
-                    nc.scalar.copy(out=bias[:, NB * i : NB * (i + 1)], in_=bp[:])
+        def spread_bias(c):
+            spread = psum_bias.tile([P, BANK], F32, name="spread")
+            nc.tensor.matmul(
+                out=spread[:], lhsT=ones[:], rhs=bias_row[:, BANK * c : BANK * (c + 1)], start=True, stop=True
+            )
+            nc.vector.tensor_copy(out=bias[:, BANK * c : BANK * (c + 1)], in_=spread[:])
 
-        stored = [0, 0, 0]
-        for c in range(len(GROUPS)):
-            col0, ncol = GROUPS[c]
-            for g in range(ROW_PASSES, PASSES):
-                multiply(g, c)
-
-            seg0 = col0 // HS
-            nseg = ncol // HS
-            acc_seg = acc[c][:].rearrange("p (s f) -> p s f", f=HS)
-            bias_seg = bias[:, col0 : col0 + ncol].rearrange("p (s f) -> p s f", f=HS)
-            spans = {}
-            for t in (2, 0, 1):
-                first = (t - seg0) % 3
-                nh = len(range(first, nseg, 3))
-                h0 = (seg0 + first) // 3
-                spans[t] = (h0, nh)
+        def finish_bank(c):
+            acc_segments = acc[c][:].rearrange("p (s f) -> p s f", f=HEAD_SIZE)
+            bias_segments = bias[:, BANK * c : BANK * (c + 1)].rearrange("p (s f) -> p s f", f=HEAD_SIZE)
+            heads = {}
+            for kind in (VALUE, QUERY, KEY):
+                first = (kind - SEGMENTS * c) % 3
+                count = len(range(first, SEGMENTS, 3))
+                h0 = (SEGMENTS * c + first) // 3
+                heads[kind] = (h0, count)
                 nc.vector.tensor_tensor(
-                    out=res[:, t, h0 : h0 + nh, :],
-                    in0=acc_seg[:, first:nseg:3, :],
-                    in1=bias_seg[:, first:nseg:3, :],
+                    out=result[:, kind, h0 : h0 + count, :],
+                    in0=acc_segments[:, first:SEGMENTS:3, :],
+                    in1=bias_segments[:, first:SEGMENTS:3, :],
                     op=ADD,
                 )
-            prods = {}
-            for t in range(2):
-                h0, nh = spans[t]
-                prod = work.tile([P, 3, ROT, 2], F32, name="prod%d" % t)
+            products = {}
+            for kind in (QUERY, KEY):
+                h0, count = heads[kind]
+                products[kind] = work.tile([P, 3, ROTARY, 2], F32, name="products%d" % kind)
                 nc.vector.tensor_tensor(
-                    out=prod[:, 0:nh, :, :],
-                    in0=res[:, t, h0 : h0 + nh, 0:ROT].unsqueeze(3).to_broadcast([P, nh, ROT, 2]),
-                    in1=rot[:].unsqueeze(1).to_broadcast([P, nh, ROT, 2]),
+                    out=products[kind][:, 0:count, :, :],
+                    in0=result[:, kind, h0 : h0 + count, 0:ROTARY]
+                    .unsqueeze(3)
+                    .to_broadcast([P, count, ROTARY, 2]),
+                    in1=rotation[:].unsqueeze(1).to_broadcast([P, count, ROTARY, 2]),
                     op=MULT,
                 )
-                prods[t] = prod
-            for t in range(2):
-                h0, nh = spans[t]
+            for kind in (QUERY, KEY):
+                h0, count = heads[kind]
                 nc.vector.tensor_tensor(
-                    out=res[:, t, h0 : h0 + nh, 0:ROT].rearrange("p h (j e) -> p h j e", e=2),
-                    in0=prods[t][:, 0:nh, 0:HALF, :],
-                    in1=prods[t][:, 0:nh, HALF:ROT, :],
+                    out=result[:, kind, h0 : h0 + count, 0:ROTARY].rearrange("p h (j e) -> p h j e", e=2),
+                    in0=products[kind][:, 0:count, 0:HALF, :],
+                    in1=products[kind][:, 0:count, HALF:ROTARY, :],
                     op=ADD,
                 )
+            return heads
+
+        nc.scalar.dma_start(out=cos_sb[:], in_=cos)
+        nc.scalar.dma_start(out=sin_sb[:], in_=sin)
+
+        nc.vector.memset(x_planes[:].bitcast(I32), 0)
+        sync_planes = []
+        for g0, g1 in SYNC_SCALES:
+            sync_planes.append(new_planes(g0, g1))
+        nc.vector.memset(bias_row[:], 0.0)
+        nc.vector.memset(ones[:], 1.0)
+        gpsimd_planes = []
+        for g0, g1 in GPSIMD_SCALES:
+            gpsimd_planes.append(new_planes(g0, g1))
+        nc.scalar.dma_start(out=bias_row[8:9, :], in_=b_qkv.rearrange("(o n) -> o n", o=1))
+
+        nc.vector.tensor_copy(out=rotation[:, 0:HALF, 0], in_=cos_sb[:])
+        nc.vector.tensor_copy(out=rotation[:, 0:HALF, 1], in_=sin_sb[:])
+        nc.vector.tensor_scalar(
+            out=rotation[:, HALF:ROTARY, 0], in0=sin_sb[:], scalar1=-1.0, scalar2=None, op0=MULT
+        )
+        nc.vector.tensor_copy(out=rotation[:, HALF:ROTARY, 1], in_=cos_sb[:])
+
+        load_x_codes(0, FIRST_X_PASSES)
+        load_row_pass(0)
+        load_scale_rows(nc.sync, I32, x_planes, x_scales, 0, PASSES)
+        for planes, (g0, g1) in zip(sync_planes, SYNC_SCALES):
+            load_scale_rows(nc.sync, I32, planes, w_qkv_scales, g0, g1)
+        for planes, (g0, g1) in zip(gpsimd_planes, GPSIMD_SCALES):
+            load_scale_rows(nc.gpsimd, F32, planes, w_qkv_scales, g0, g1)
+        load_x_codes(FIRST_X_PASSES, PASSES)
+        for g in range(1, ROW_PASSES):
+            load_row_pass(g)
+        for c in range(BANKS):
+            load_bank_passes(c)
+
+        for g in range(ROW_PASSES):
+            for c in range(BANKS):
+                multiply(g, c)
+            if g < BANKS:
+                spread_bias(g)
+            if g in LATE_GPSIMD_SCALES:
+                g0, g1 = LATE_GPSIMD_SCALES[g]
+                load_scale_rows(nc.gpsimd, F32, new_planes(g0, g1), w_qkv_scales, g0, g1)
+
+        stored = [0, 0, 0]
+        for c in range(BANKS):
+            for g in range(ROW_PASSES, PASSES):
+                multiply(g, c)
+            heads = finish_bank(c)
             if c in STORE_AFTER:
-                for t in (2, 0, 1):
-                    h1 = spans[t][0] + spans[t][1]
-                    queues[STORE_QUEUES[c][t]].dma_start(
-                        out=outs[t][0, :, stored[t] : h1, :], in_=res[:, t, stored[t] : h1, :]
+                for kind in (VALUE, QUERY, KEY):
+                    done = heads[kind][0] + heads[kind][1]
+                    queue = nc.sync if kind == QUERY else nc.scalar
+                    queue.dma_start(
+                        out=outs[kind][0, :, stored[kind] : done, :],
+                        in_=result[:, kind, stored[kind] : done, :],
                     )
-                    stored[t] = h1
+                    stored[kind] = done

@@ -25,10 +25,8 @@ SEGMENTS = BANK // HEAD_SIZE
 FLOPS = 2 * P * 512 * PASSES * WIDTH
 
 ROW_PASSES = 11
+GROUPS = ((0, 512), (512, 512), (1024, 512), (1536, 512), (2048, 512), (2560, 512))
 FIRST_X_PASSES = 4
-SYNC_SCALES = ((0, 1), (1, 2))
-GPSIMD_SCALES = ((2, 4), (4, 8))
-LATE_GPSIMD_SCALES = {0: (8, 12), 2: (12, 16)}
 STORE_AFTER = (2, 4, 5)
 
 
@@ -52,12 +50,13 @@ def tile_gptneoxattention_pa_kernel(
         rotation = keep.tile([P, ROTARY, 2], F32, name="rotation")
         bias_row = keep.tile([P, WIDTH], BF16, name="bias_row")
         ones = keep.tile([P, P], BF16, name="ones")
+        warm = keep.tile([P, 1], F32, name="warm")
         bias = keep.tile([P, WIDTH], F32, name="bias")
         result = keep.tile([P, 3, HEADS, HEAD_SIZE], F32, name="result")
         acc = []
-        for c in range(BANKS):
-            acc_c = psum.tile([P, BANK], F32, name="acc%d" % c)
-            acc.append(acc_c)
+        for i in range(len(GROUPS)):
+            acc_i = psum.tile([P, BANK], F32, name="acc%d" % i)
+            acc.append(acc_i)
 
         w_plane = {}
         w_codes = {}
@@ -69,11 +68,11 @@ def tile_gptneoxattention_pa_kernel(
                 w_plane[g] = planes[:, g - g0, :]
             return planes
 
-        def load_scale_rows(queue, word, planes, scales, g0, g1):
+        def load_scale_rows(planes, scales, g0, g1):
             for r in range(4):
-                queue.dma_start(
-                    out=planes[r:P:32, :, :].bitcast(word),
-                    in_=scales[g0:g1, r:16:4, :].rearrange("g q n -> q g n").bitcast(word),
+                nc.sync.dma_start(
+                    out=planes[r:P:32, :, :].bitcast(I32),
+                    in_=scales[g0:g1, r:16:4, :].rearrange("g q n -> q g n").bitcast(I32),
                 )
 
         def load_x_codes(g0, g1):
@@ -85,27 +84,29 @@ def tile_gptneoxattention_pa_kernel(
         def load_row_pass(g):
             codes = keep.tile([P, 2 * WIDTH], U8, name="w_row%d" % g, align_bytes=64)
             nc.sync.dma_start(out=codes[:].bitcast(I32), in_=w_qkv_words[g].bitcast(I32))
-            for c in range(BANKS):
-                w_codes[(c, g)] = codes[:, 2 * BANK * c : 2 * BANK * (c + 1)]
+            for i, (col0, width) in enumerate(GROUPS):
+                w_codes[(i, g)] = codes[:, 2 * col0 : 2 * (col0 + width)]
 
-        def load_bank_passes(c):
-            codes = keep.tile([P, PASSES - ROW_PASSES, 2 * BANK], U8, name="w_bank%d" % c, align_bytes=64)
+        def load_group_passes(i):
+            col0, width = GROUPS[i]
+            codes = keep.tile([P, PASSES - ROW_PASSES, 2 * width], U8, name="w_group%d" % i, align_bytes=64)
             nc.sync.dma_start(
                 out=codes[:].bitcast(I32),
-                in_=w_qkv_words[ROW_PASSES:PASSES, :, 2 * BANK * c : 2 * BANK * (c + 1)]
+                in_=w_qkv_words[ROW_PASSES:PASSES, :, 2 * col0 : 2 * (col0 + width)]
                 .rearrange("g p n -> p g n")
                 .bitcast(I32),
             )
             for g in range(ROW_PASSES, PASSES):
-                w_codes[(c, g)] = codes[:, g - ROW_PASSES, :]
+                w_codes[(i, g)] = codes[:, g - ROW_PASSES, :]
 
-        def multiply(g, c):
+        def multiply(g, i):
+            col0, width = GROUPS[i]
             nc.tensor.matmul_mx(
-                out=acc[c][:],
+                out=acc[i][:, 0:width],
                 lhsT=x_codes[:, g, :].bitcast(FP4X4),
                 lhsT_scale=x_planes[:, g, :],
-                rhs=w_codes[(c, g)].bitcast(FP4X4),
-                rhs_scale=w_plane[g][:, BANK * c : BANK * (c + 1)],
+                rhs=w_codes[(i, g)].bitcast(FP4X4),
+                rhs_scale=w_plane[g][:, col0 : col0 + width],
                 start=(g == 0),
                 stop=(g == PASSES - 1),
             )
@@ -115,25 +116,36 @@ def tile_gptneoxattention_pa_kernel(
             nc.tensor.matmul(
                 out=spread[:], lhsT=ones[:], rhs=bias_row[:, BANK * c : BANK * (c + 1)], start=True, stop=True
             )
-            nc.vector.tensor_copy(out=bias[:, BANK * c : BANK * (c + 1)], in_=spread[:])
+            nc.scalar.copy(out=bias[:, BANK * c : BANK * (c + 1)], in_=spread[:])
 
-        def finish_bank(c):
-            acc_segments = acc[c][:].rearrange("p (s f) -> p s f", f=HEAD_SIZE)
-            bias_segments = bias[:, BANK * c : BANK * (c + 1)].rearrange("p (s f) -> p s f", f=HEAD_SIZE)
+        done = [0, 0, 0]
+        stored = [0, 0, 0]
+
+        def finish_group(i):
+            col0, width = GROUPS[i]
+            s0 = col0 // HEAD_SIZE
+            segments = width // HEAD_SIZE
+            acc_segments = acc[i][:, 0:width].rearrange("p (s f) -> p s f", f=HEAD_SIZE)
+            bias_segments = bias[:, col0 : col0 + width].rearrange("p (s f) -> p s f", f=HEAD_SIZE)
             heads = {}
             for kind in (VALUE, QUERY, KEY):
-                first = (kind - SEGMENTS * c) % 3
-                count = len(range(first, SEGMENTS, 3))
-                h0 = (SEGMENTS * c + first) // 3
+                first = (kind - s0) % 3
+                count = len(range(first, segments, 3))
+                if count == 0:
+                    continue
+                h0 = (s0 + first) // 3
                 heads[kind] = (h0, count)
+                done[kind] = h0 + count
                 nc.vector.tensor_tensor(
                     out=result[:, kind, h0 : h0 + count, :],
-                    in0=acc_segments[:, first:SEGMENTS:3, :],
-                    in1=bias_segments[:, first:SEGMENTS:3, :],
+                    in0=acc_segments[:, first:segments:3, :],
+                    in1=bias_segments[:, first:segments:3, :],
                     op=ADD,
                 )
             products = {}
             for kind in (QUERY, KEY):
+                if kind not in heads:
+                    continue
                 h0, count = heads[kind]
                 products[kind] = work.tile([P, 3, ROTARY, 2], F32, name="products%d" % kind)
                 nc.vector.tensor_tensor(
@@ -145,6 +157,8 @@ def tile_gptneoxattention_pa_kernel(
                     op=MULT,
                 )
             for kind in (QUERY, KEY):
+                if kind not in heads:
+                    continue
                 h0, count = heads[kind]
                 nc.vector.tensor_tensor(
                     out=result[:, kind, h0 : h0 + count, 0:ROTARY].rearrange("p h (j e) -> p h j e", e=2),
@@ -152,21 +166,33 @@ def tile_gptneoxattention_pa_kernel(
                     in1=products[kind][:, 0:count, HALF:ROTARY, :],
                     op=ADD,
                 )
-            return heads
 
-        nc.scalar.dma_start(out=cos_sb[:], in_=cos)
-        nc.scalar.dma_start(out=sin_sb[:], in_=sin)
-
-        nc.vector.memset(x_planes[:].bitcast(I32), 0)
-        sync_planes = []
-        for g0, g1 in SYNC_SCALES:
-            sync_planes.append(new_planes(g0, g1))
-        nc.vector.memset(bias_row[:], 0.0)
         nc.vector.memset(ones[:], 1.0)
-        gpsimd_planes = []
-        for g0, g1 in GPSIMD_SCALES:
-            gpsimd_planes.append(new_planes(g0, g1))
-        nc.scalar.dma_start(out=bias_row[8:9, :], in_=b_qkv.rearrange("(o n) -> o n", o=1))
+        nc.scalar.copy(out=warm[:], in_=ones[:, 0:1])
+        nc.vector.memset(x_planes[:].bitcast(I32), 0)
+        nc.vector.memset(bias_row[:], 0.0)
+        bounds = [(PASSES * g) // ROW_PASSES for g in range(ROW_PASSES + 1)]
+        slot_planes = []
+        for g in range(ROW_PASSES):
+            slot_planes.append(new_planes(bounds[g], bounds[g + 1]))
+
+        load_x_codes(0, FIRST_X_PASSES)
+        load_row_pass(0)
+        load_scale_rows(x_planes, x_scales, 0, PASSES)
+        load_row_pass(1)
+        load_scale_rows(slot_planes[0], w_qkv_scales, bounds[0], bounds[1])
+        load_x_codes(FIRST_X_PASSES, PASSES)
+        for g in range(1, ROW_PASSES):
+            load_scale_rows(slot_planes[g], w_qkv_scales, bounds[g], bounds[g + 1])
+            if g + 1 < ROW_PASSES:
+                load_row_pass(g + 1)
+            if g == 1:
+                nc.scalar.dma_start(out=bias_row[8:9, :], in_=b_qkv.rearrange("(o n) -> o n", o=1))
+            if g == 2:
+                nc.scalar.dma_start(out=cos_sb[:], in_=cos)
+                nc.scalar.dma_start(out=sin_sb[:], in_=sin)
+        for i in range(len(GROUPS)):
+            load_group_passes(i)
 
         nc.vector.tensor_copy(out=rotation[:, 0:HALF, 0], in_=cos_sb[:])
         nc.vector.tensor_copy(out=rotation[:, 0:HALF, 1], in_=sin_sb[:])
@@ -175,39 +201,22 @@ def tile_gptneoxattention_pa_kernel(
         )
         nc.vector.tensor_copy(out=rotation[:, HALF:ROTARY, 1], in_=cos_sb[:])
 
-        load_x_codes(0, FIRST_X_PASSES)
-        load_row_pass(0)
-        load_scale_rows(nc.sync, I32, x_planes, x_scales, 0, PASSES)
-        for planes, (g0, g1) in zip(sync_planes, SYNC_SCALES):
-            load_scale_rows(nc.sync, I32, planes, w_qkv_scales, g0, g1)
-        for planes, (g0, g1) in zip(gpsimd_planes, GPSIMD_SCALES):
-            load_scale_rows(nc.gpsimd, F32, planes, w_qkv_scales, g0, g1)
-        load_x_codes(FIRST_X_PASSES, PASSES)
-        for g in range(1, ROW_PASSES):
-            load_row_pass(g)
-        for c in range(BANKS):
-            load_bank_passes(c)
-
         for g in range(ROW_PASSES):
-            for c in range(BANKS):
-                multiply(g, c)
-            if g < BANKS:
-                spread_bias(g)
-            if g in LATE_GPSIMD_SCALES:
-                g0, g1 = LATE_GPSIMD_SCALES[g]
-                load_scale_rows(nc.gpsimd, F32, new_planes(g0, g1), w_qkv_scales, g0, g1)
+            for i in range(len(GROUPS)):
+                multiply(g, i)
+            if 1 <= g <= BANKS:
+                spread_bias(g - 1)
 
-        stored = [0, 0, 0]
-        for c in range(BANKS):
+        for i in range(len(GROUPS)):
             for g in range(ROW_PASSES, PASSES):
-                multiply(g, c)
-            heads = finish_bank(c)
-            if c in STORE_AFTER:
+                multiply(g, i)
+            finish_group(i)
+            if i in STORE_AFTER:
                 for kind in (VALUE, QUERY, KEY):
-                    done = heads[kind][0] + heads[kind][1]
-                    queue = nc.sync if kind == QUERY else nc.scalar
-                    queue.dma_start(
-                        out=outs[kind][0, :, stored[kind] : done, :],
-                        in_=result[:, kind, stored[kind] : done, :],
-                    )
-                    stored[kind] = done
+                    if done[kind] > stored[kind]:
+                        queue = nc.sync if kind == QUERY else nc.scalar
+                        queue.dma_start(
+                            out=outs[kind][0, :, stored[kind] : done[kind], :],
+                            in_=result[:, kind, stored[kind] : done[kind], :],
+                        )
+                        stored[kind] = done[kind]

@@ -26,7 +26,7 @@ FLOPS = 2 * P * 512 * PASSES * WIDTH
 
 ROW_PASSES = 11
 GROUPS = ((0, 512), (512, 512), (1024, 512), (1536, 512), (2048, 512), (2560, 512))
-FIRST_X_PASSES = 4
+SCALE_RANGES = ((0, 8), (8, 16))
 STORE_AFTER = (2, 4, 5)
 
 
@@ -74,6 +74,16 @@ def tile_gptneoxattention_pa_kernel(
                     out=planes[r:P:32, :, :].bitcast(I32),
                     in_=scales[g0:g1, r:16:4, :].rearrange("g q n -> q g n").bitcast(I32),
                 )
+
+        def load_scale_partitions(planes, scales, g0, g1):
+            for r in range(4):
+                for quadrant in (0, 2, 1, 3):
+                    q = 4 * quadrant + r
+                    p0 = 32 * quadrant + r
+                    nc.sync.dma_start(
+                        out=planes[p0 : p0 + 1, :, :].bitcast(I32),
+                        in_=scales[g0:g1, q : q + 1, :].rearrange("g q n -> q g n").bitcast(I32),
+                    )
 
         def load_x_codes(g0, g1):
             nc.sync.dma_start(
@@ -170,27 +180,24 @@ def tile_gptneoxattention_pa_kernel(
         nc.vector.memset(ones[:], 1.0)
         nc.scalar.copy(out=warm[:], in_=ones[:, 0:1])
         nc.vector.memset(x_planes[:].bitcast(I32), 0)
-        nc.vector.memset(bias_row[:], 0.0)
-        bounds = [(PASSES * g) // ROW_PASSES for g in range(ROW_PASSES + 1)]
-        slot_planes = []
-        for g in range(ROW_PASSES):
-            slot_planes.append(new_planes(bounds[g], bounds[g + 1]))
+        range_planes = []
+        for g0, g1 in SCALE_RANGES:
+            range_planes.append(new_planes(g0, g1))
+            if g0 == 0:
+                nc.vector.memset(bias_row[:], 0.0)
 
-        load_x_codes(0, FIRST_X_PASSES)
+        load_x_codes(0, PASSES)
         load_row_pass(0)
-        load_scale_rows(x_planes, x_scales, 0, PASSES)
         load_row_pass(1)
-        load_scale_rows(slot_planes[0], w_qkv_scales, bounds[0], bounds[1])
-        load_x_codes(FIRST_X_PASSES, PASSES)
-        for g in range(1, ROW_PASSES):
-            load_scale_rows(slot_planes[g], w_qkv_scales, bounds[g], bounds[g + 1])
-            if g + 1 < ROW_PASSES:
-                load_row_pass(g + 1)
-            if g == 1:
-                nc.scalar.dma_start(out=bias_row[8:9, :], in_=b_qkv.rearrange("(o n) -> o n", o=1))
-            if g == 2:
-                nc.scalar.dma_start(out=cos_sb[:], in_=cos)
-                nc.scalar.dma_start(out=sin_sb[:], in_=sin)
+        load_scale_rows(x_planes, x_scales, 0, PASSES)
+        load_scale_partitions(range_planes[0], w_qkv_scales, 0, 8)
+        nc.scalar.dma_start(out=bias_row[8:9, :], in_=b_qkv.rearrange("(o n) -> o n", o=1))
+        nc.scalar.dma_start(out=cos_sb[:], in_=cos)
+        nc.scalar.dma_start(out=sin_sb[:], in_=sin)
+        for g in range(2, ROW_PASSES):
+            if g == 6:
+                load_scale_partitions(range_planes[1], w_qkv_scales, 8, 16)
+            load_row_pass(g)
         for i in range(len(GROUPS)):
             load_group_passes(i)
 

@@ -97,17 +97,17 @@ def tile_gptneoxattention_pa_kernel(
             for i, (col0, width) in enumerate(GROUPS):
                 w_codes[(i, g)] = codes[:, 2 * col0 : 2 * (col0 + width)]
 
-        def load_group_passes(i):
+        def load_group_passes(i, g0, g1):
             col0, width = GROUPS[i]
-            codes = keep.tile([P, PASSES - ROW_PASSES, 2 * width], U8, name="w_group%d" % i, align_bytes=64)
+            codes = keep.tile([P, g1 - g0, 2 * width], U8, name="w_group%d_%d" % (i, g0), align_bytes=64)
             nc.sync.dma_start(
                 out=codes[:].bitcast(I32),
-                in_=w_qkv_words[ROW_PASSES:PASSES, :, 2 * col0 : 2 * (col0 + width)]
+                in_=w_qkv_words[g0:g1, :, 2 * col0 : 2 * (col0 + width)]
                 .rearrange("g p n -> p g n")
                 .bitcast(I32),
             )
-            for g in range(ROW_PASSES, PASSES):
-                w_codes[(i, g)] = codes[:, g - ROW_PASSES, :]
+            for g in range(g0, g1):
+                w_codes[(i, g)] = codes[:, g - g0, :]
 
         def multiply(g, i):
             col0, width = GROUPS[i]
@@ -198,8 +198,10 @@ def tile_gptneoxattention_pa_kernel(
             if g == 6:
                 load_scale_partitions(range_planes[1], w_qkv_scales, 8, 16)
             load_row_pass(g)
-        for i in range(len(GROUPS)):
-            load_group_passes(i)
+        for i in range(len(GROUPS) - 1):
+            load_group_passes(i, ROW_PASSES, PASSES)
+        load_group_passes(len(GROUPS) - 1, ROW_PASSES, PASSES - 1)
+        load_group_passes(len(GROUPS) - 1, PASSES - 1, PASSES)
 
         nc.vector.tensor_copy(out=rotation[:, 0:HALF, 0], in_=cos_sb[:])
         nc.vector.tensor_copy(out=rotation[:, 0:HALF, 1], in_=sin_sb[:])

@@ -223,7 +223,7 @@ def tile_gptneoxattention_pa_kernel(
             if i in STORE_AFTER:
                 for kind in (VALUE, QUERY, KEY):
                     if done[kind] > stored[kind]:
-                        queue = nc.sync if kind == QUERY else nc.scalar
+                        queue = nc.scalar if i == len(GROUPS) - 1 else nc.sync
                         queue.dma_start(
                             out=outs[kind][0, :, stored[kind] : done[kind], :],
                             in_=result[:, kind, stored[kind] : done[kind], :],

@@ -26,6 +26,7 @@ FLOPS = 2 * P * 512 * PASSES * WIDTH
 
 ROW_PASSES = 11
 GROUPS = ((0, 512), (512, 512), (1024, 512), (1536, 512), (2048, 512), (2560, 512))
+GROUP_CUT = 14
 SCALE_RANGES = ((0, 8), (8, 16))
 STORE_AFTER = (2, 4, 5)
 
@@ -198,10 +199,9 @@ def tile_gptneoxattention_pa_kernel(
             if g == 6:
                 load_scale_partitions(range_planes[1], w_qkv_scales, 8, 16)
             load_row_pass(g)
-        for i in range(len(GROUPS) - 1):
-            load_group_passes(i, ROW_PASSES, PASSES)
-        load_group_passes(len(GROUPS) - 1, ROW_PASSES, PASSES - 1)
-        load_group_passes(len(GROUPS) - 1, PASSES - 1, PASSES)
+        for i in range(len(GROUPS)):
+            load_group_passes(i, ROW_PASSES, GROUP_CUT)
+            load_group_passes(i, GROUP_CUT, PASSES)
 
         nc.vector.tensor_copy(out=rotation[:, 0:HALF, 0], in_=cos_sb[:])
         nc.vector.tensor_copy(out=rotation[:, 0:HALF, 1], in_=sin_sb[:])

from contextlib import ExitStack

import concourse.mybir as mybir

F32 = mybir.dt.float32
BF16 = mybir.dt.bfloat16
I32 = mybir.dt.int32
U8 = mybir.dt.uint8
FP4X4 = mybir.dt.float4_e2m1fn_x4
ADD = mybir.AluOpType.add
MULT = mybir.AluOpType.mult

P = 128
PASSES = 16
WIDTH = 3072
HEADS = 16
HEAD_SIZE = 64
ROTARY = 32
HALF = ROTARY // 2
QUERY, KEY, VALUE = 0, 1, 2
BANK = 512
BANKS = WIDTH // BANK
SEGMENTS = BANK // HEAD_SIZE

FLOPS = 2 * P * 512 * PASSES * WIDTH

ROW_PASSES = 11
GROUPS = ((0, 512), (512, 512), (1024, 512), (1536, 512), (2048, 512), (2560, 512))
GROUP_CUT = 14
SCALE_RANGES = ((0, 8), (8, 16))
STORE_AFTER = (2, 4, 5)


def tile_gptneoxattention_pa_kernel(
    tc, x_words, x_scales, w_qkv_words, w_qkv_scales, b_qkv, cos, sin, out_0, out_1, out_2
):
    nc = tc.nc
    outs = (out_0, out_1, out_2)

    with ExitStack() as ctx:
        keep = ctx.enter_context(tc.tile_pool(name="keep", bufs=1))
        work = ctx.enter_context(tc.tile_pool(name="work", bufs=2))
        psum = ctx.enter_context(tc.psum_pool(name="psum", bufs=1))
        psum_bias = ctx.enter_context(tc.psum_pool(name="psum_bias", bufs=2))
        ctx.enter_context(tc.manual_schedule())

        x_codes = keep.tile([P, PASSES, 2 * P], U8, name="x_codes", align_bytes=64)
        x_planes = keep.tile([P, PASSES, P], U8, name="x_planes", align_bytes=64)
        cos_sb = keep.tile([P, HALF], BF16, name="cos_sb")
        sin_sb = keep.tile([P, HALF], BF16, name="sin_sb")
        rotation = keep.tile([P, ROTARY, 2], F32, name="rotation")
        bias_row = keep.tile([P, WIDTH], BF16, name="bias_row")
        ones = keep.tile([P, P], BF16, name="ones")
        warm = keep.tile([P, 1], F32, name="warm")
        bias = keep.tile([P, WIDTH], F32, name="bias")
        result = keep.tile([P, 3, HEADS, HEAD_SIZE], F32, name="result")
        acc = []
        for i in range(len(GROUPS)):
            acc_i = psum.tile([P, BANK], F32, name="acc%d" % i)
            acc.append(acc_i)

        w_plane = {}
        w_codes = {}

        def new_planes(g0, g1):
            planes = keep.tile([P, g1 - g0, WIDTH], U8, name="w_planes%d" % g0, align_bytes=64)
            nc.vector.memset(planes[:].bitcast(I32), 0)
            for g in range(g0, g1):
                w_plane[g] = planes[:, g - g0, :]
            return planes

        def load_scale_rows(planes, scales, g0, g1):
            for r in range(4):
                nc.sync.dma_start(
                    out=planes[r:P:32, :, :].bitcast(I32),
                    in_=scales[g0:g1, r:16:4, :].rearrange("g q n -> q g n").bitcast(I32),
                )

        def load_scale_partitions(planes, scales, g0, g1):
            for r in range(4):
                for quadrant in (0, 2, 1, 3):
                    q = 4 * quadrant + r
                    p0 = 32 * quadrant + r
                    nc.sync.dma_start(
                        out=planes[p0 : p0 + 1, :, :].bitcast(I32),
                        in_=scales[g0:g1, q : q + 1, :].rearrange("g q n -> q g n").bitcast(I32),
                    )

        def load_x_codes(g0, g1):
            nc.sync.dma_start(
                out=x_codes[:, g0:g1, :].bitcast(I32),
                in_=x_words[g0:g1].rearrange("g p n -> p g n").bitcast(I32),
            )

        def load_row_pass(g):
            codes = keep.tile([P, 2 * WIDTH], U8, name="w_row%d" % g, align_bytes=64)
            nc.sync.dma_start(out=codes[:].bitcast(I32), in_=w_qkv_words[g].bitcast(I32))
            for i, (col0, width) in enumerate(GROUPS):
                w_codes[(i, g)] = codes[:, 2 * col0 : 2 * (col0 + width)]

        def load_group_passes(i, g0, g1):
            col0, width = GROUPS[i]
            codes = keep.tile([P, g1 - g0, 2 * width], U8, name="w_group%d_%d" % (i, g0), align_bytes=64)
            nc.sync.dma_start(
                out=codes[:].bitcast(I32),
                in_=w_qkv_words[g0:g1, :, 2 * col0 : 2 * (col0 + width)]
                .rearrange("g p n -> p g n")
                .bitcast(I32),
            )
            for g in range(g0, g1):
                w_codes[(i, g)] = codes[:, g - g0, :]

        def multiply(g, i):
            col0, width = GROUPS[i]
            nc.tensor.matmul_mx(
                out=acc[i][:, 0:width],
                lhsT=x_codes[:, g, :].bitcast(FP4X4),
                lhsT_scale=x_planes[:, g, :],
                rhs=w_codes[(i, g)].bitcast(FP4X4),
                rhs_scale=w_plane[g][:, col0 : col0 + width],
                start=(g == 0),
                stop=(g == PASSES - 1),
            )

        def spread_bias(c):
            spread = psum_bias.tile([P, BANK], F32, name="spread")
            nc.tensor.matmul(
                out=spread[:], lhsT=ones[:], rhs=bias_row[:, BANK * c : BANK * (c + 1)], start=True, stop=True
            )
            nc.scalar.copy(out=bias[:, BANK * c : BANK * (c + 1)], in_=spread[:])

        done = [0, 0, 0]
        stored = [0, 0, 0]

        def finish_group(i):
            col0, width = GROUPS[i]
            s0 = col0 // HEAD_SIZE
            segments = width // HEAD_SIZE
            acc_segments = acc[i][:, 0:width].rearrange("p (s f) -> p s f", f=HEAD_SIZE)
            bias_segments = bias[:, col0 : col0 + width].rearrange("p (s f) -> p s f", f=HEAD_SIZE)
            heads = {}
            for kind in (VALUE, QUERY, KEY):
                first = (kind - s0) % 3
                count = len(range(first, segments, 3))
                if count == 0:
                    continue
                h0 = (s0 + first) // 3
                heads[kind] = (h0, count)
                done[kind] = h0 + count
                nc.vector.tensor_tensor(
                    out=result[:, kind, h0 : h0 + count, :],
                    in0=acc_segments[:, first:segments:3, :],
                    in1=bias_segments[:, first:segments:3, :],
                    op=ADD,
                )
            products = {}
            for kind in (QUERY, KEY):
                if kind not in heads:
                    continue
                h0, count = heads[kind]
                products[kind] = work.tile([P, 3, ROTARY, 2], F32, name="products%d" % kind)
                nc.vector.tensor_tensor(
                    out=products[kind][:, 0:count, :, :],
                    in0=result[:, kind, h0 : h0 + count, 0:ROTARY]
                    .unsqueeze(3)
                    .to_broadcast([P, count, ROTARY, 2]),
                    in1=rotation[:].unsqueeze(1).to_broadcast([P, count, ROTARY, 2]),
                    op=MULT,
                )
            for kind in (QUERY, KEY):
                if kind not in heads:
                    continue
                h0, count = heads[kind]
                nc.vector.tensor_tensor(
                    out=result[:, kind, h0 : h0 + count, 0:ROTARY].rearrange("p h (j e) -> p h j e", e=2),
                    in0=products[kind][:, 0:count, 0:HALF, :],
                    in1=products[kind][:, 0:count, HALF:ROTARY, :],
                    op=ADD,
                )

        nc.vector.memset(ones[:], 1.0)
        nc.scalar.copy(out=warm[:], in_=ones[:, 0:1])
        nc.vector.memset(x_planes[:].bitcast(I32), 0)
        range_planes = []
        for g0, g1 in SCALE_RANGES:
            range_planes.append(new_planes(g0, g1))
            if g0 == 0:
                nc.vector.memset(bias_row[:], 0.0)

        load_x_codes(0, PASSES)
        load_row_pass(0)
        load_row_pass(1)
        load_scale_rows(x_planes, x_scales, 0, PASSES)
        load_scale_partitions(range_planes[0], w_qkv_scales, 0, 8)
        nc.scalar.dma_start(out=bias_row[8:9, :], in_=b_qkv.rearrange("(o n) -> o n", o=1))
        nc.scalar.dma_start(out=cos_sb[:], in_=cos)
        nc.scalar.dma_start(out=sin_sb[:], in_=sin)
        for g in range(2, ROW_PASSES):
            if g == 6:
                load_scale_partitions(range_planes[1], w_qkv_scales, 8, 16)
            load_row_pass(g)
        for i in range(len(GROUPS)):
            load_group_passes(i, ROW_PASSES, GROUP_CUT)
            load_group_passes(i, GROUP_CUT, PASSES)

        nc.vector.tensor_copy(out=rotation[:, 0:HALF, 0], in_=cos_sb[:])
        nc.vector.tensor_copy(out=rotation[:, 0:HALF, 1], in_=sin_sb[:])
        nc.vector.tensor_scalar(
            out=rotation[:, HALF:ROTARY, 0], in0=sin_sb[:], scalar1=-1.0, scalar2=None, op0=MULT
        )
        nc.vector.tensor_copy(out=rotation[:, HALF:ROTARY, 1], in_=cos_sb[:])

        for g in range(ROW_PASSES):
            for i in range(len(GROUPS)):
                multiply(g, i)
            if 1 <= g <= BANKS:
                spread_bias(g - 1)

        for i in range(len(GROUPS)):
            for g in range(ROW_PASSES, PASSES):
                multiply(g, i)
            finish_group(i)
            if i in STORE_AFTER:
                for kind in (VALUE, QUERY, KEY):
                    if done[kind] > stored[kind]:
                        queue = nc.scalar if i == len(GROUPS) - 1 else nc.sync
                        queue.dma_start(
                            out=outs[kind][0, :, stored[kind] : done[kind], :],
                            in_=result[:, kind, stored[kind] : done[kind], :],
                        )
                        stored[kind] = done[kind]
